import numpy as np
import ml_dtypes


def mxq(x, axis, fmt="e4m3"):
    dtype, down = {"e4m3": (ml_dtypes.float8_e4m3fn, 7), "e5m2": (ml_dtypes.float8_e5m2, 14)}[fmt]
    v = np.moveaxis(np.asarray(x, np.float32).astype(ml_dtypes.bfloat16).astype(np.float64), axis, -1)
    blocks = v.reshape(v.shape[:-1] + (-1, 32))
    amax = np.abs(blocks).max(-1, keepdims=True)
    byte = np.maximum(np.where(amax > 0, np.frexp(amax)[1] - 1 + 127, 0) - down, 1)
    scale = np.exp2(byte - 127.0)
    codes = (blocks / scale).astype(np.float32).astype(dtype).astype(np.float64)
    return np.moveaxis((codes * scale).reshape(v.shape), -1, axis)


WIDE = False


def mx_kscale(k):
    if not WIDE:
        return np.ones(k)
    levels = np.array([10, -10, 5, -5, 0])
    a = np.random.permutation(np.resize(levels, k // 512 * 4)).reshape(k // 512, 4)
    idx = np.arange(k)
    return np.exp2(a[idx // 512, idx % 128 // 32])


BF16 = ml_dtypes.bfloat16


def bf(x):
    return np.asarray(x, np.float32).astype(BF16)


def f64(x):
    return np.asarray(x).astype(np.float64)


B, IN_F, OUT_F = 512, 16384, 512
EPS = 1e-5


def setup_inputs():
    s = mx_kscale(IN_F)
    scale = 1.0 / np.sqrt(IN_F)
    return {"x": bf(np.random.standard_normal((B, IN_F)) * s),
            "y": bf(np.random.standard_normal((B, OUT_F))),
            "weight": bf(np.random.uniform(-scale, scale, (OUT_F, IN_F)) / s[None, :]),
            "bias": bf(np.random.uniform(-0.5, 0.5, OUT_F)),
            "running_mean": bf(np.random.standard_normal(OUT_F) * 0.3),
            "running_var": bf(np.random.uniform(0.5, 1.5, OUT_F)),
            "norm_weight": bf(1.0 + 0.1 * np.random.standard_normal(OUT_F)),
            "norm_bias": bf(np.random.standard_normal(OUT_F) * 0.3)}


def reference(x, y, weight, bias, running_mean, running_var, norm_weight, norm_bias):
    linear = (mxq(f64(x), 1, "e4m3") @ mxq(f64(weight), 1, "e4m3").T) + f64(bias)
    inv_std = 1.0 / np.sqrt(f64(running_var) + EPS)
    norm = (linear - f64(running_mean)) * inv_std * f64(norm_weight) + f64(norm_bias)
    return (norm + f64(y)) * f64(y)

@@ -1,0 +1,212 @@
+from contextlib import ExitStack
+
+import concourse.mybir as mybir
+from concourse.masks import make_identity
+
+F32 = mybir.dt.float32
+BF16 = mybir.dt.bfloat16
+U32 = mybir.dt.uint32
+U8 = mybir.dt.uint8
+FP8X4 = mybir.dt.float8_e4m3fn_x4
+SQRT = mybir.ActivationFunctionType.Sqrt
+
+P = 128
+PACK = 4
+K_PASS = P * PACK
+BANK = 512
+
+ROWS = 512
+FEATURES = 512
+K = 16384
+EPS = 1e-5
+BLOCKS = ROWS // P
+PASSES = K // K_PASS
+WORDS = K_PASS // 2
+PER_PARTITION = FEATURES // P
+
+CHUNK_MAX = 2048
+PREFETCH = 4
+LAG = 2
+
+FLOPS = 2 * ROWS * FEATURES * K
+
+
+def chunk_widths():
+    widths = [K_PASS]
+    while sum(widths) < K:
+        widths.append(min(sum(widths), CHUNK_MAX))
+    assert sum(widths) == K
+    return widths
+
+
+def tile_modelnew_k_kernel(
+    tc, x, y, weight, bias, running_mean, running_var, norm_weight, norm_bias, out
+):
+    nc = tc.nc
+    widths = chunk_widths()
+    home = [(c, i) for c, width in enumerate(widths) for i in range(width // K_PASS)]
+    x_view = x.rearrange("(b p) k -> p b k", p=P)
+    w_view = weight.rearrange("(b p) k -> p b k", p=P)
+    y_view = y.rearrange("(b p) n -> p b n", p=P)
+
+    with ExitStack() as ctx:
+        consts = ctx.enter_context(tc.tile_pool(name="consts", bufs=1))
+        stage = ctx.enter_context(tc.tile_pool(name="stage", bufs=PREFETCH))
+        group_pool = ctx.enter_context(tc.tile_pool(name="grouped", bufs=3))
+        code_pool = ctx.enter_context(tc.tile_pool(name="codes", bufs=LAG + 1))
+        result_pool = ctx.enter_context(tc.tile_pool(name="result", bufs=BLOCKS))
+        turn_psum = ctx.enter_context(tc.psum_pool(name="turn", bufs=4))
+        acc_psum = ctx.enter_context(tc.psum_pool(name="acc", bufs=1))
+        ctx.enter_context(tc.manual_schedule())
+
+        staged = {}
+        grouped = {}
+        quantised = {}
+
+        def load_chunk(c):
+            k0, width = sum(widths[:c]), widths[c]
+            x_st = stage.tile([P, BLOCKS * width], BF16, tag="x_st")
+            nc.sync.dma_start(
+                out=x_st[:].rearrange("p (b k) -> p b k", b=BLOCKS),
+                in_=x_view[:, :, k0 : k0 + width],
+            )
+            w_st = stage.tile([P, BLOCKS * width], BF16, tag="w_st")
+            nc.sync.dma_start(
+                out=w_st[:].rearrange("p (b k) -> p b k", b=BLOCKS),
+                in_=w_view[:, :, k0 : k0 + width],
+            )
+            staged[c] = (x_st, w_st)
+
+        def load_vector(vector, name):
+            column = consts.tile([P, PER_PARTITION], BF16, name=name)
+            nc.scalar.dma_start(out=column[:], in_=vector.rearrange("(p j) -> p j", j=PER_PARTITION))
+            return column
+
+        var_col = load_vector(running_var, "var_col")
+        gain_col = load_vector(norm_weight, "gain_col")
+        bias_col = load_vector(bias, "bias_col")
+        mean_col = load_vector(running_mean, "mean_col")
+        offset_col = load_vector(norm_bias, "offset_col")
+
+        for c in range(PREFETCH):
+            load_chunk(c)
+        y_sb = consts.tile([P, BLOCKS * FEATURES], BF16)
+        nc.sync.dma_start(out=y_sb[:].rearrange("p (b n) -> p b n", b=BLOCKS), in_=y_view)
+
+        ident = consts.tile([P, P], F32)
+        make_identity(nc, ident[:])
+
+        scale_col = consts.tile([P, PER_PARTITION], F32)
+        shift_col = consts.tile([P, PER_PARTITION], F32)
+        nc.scalar.activation(out=scale_col[:], in_=var_col[:], func=SQRT, bias=EPS)
+        nc.vector.reciprocal(out=scale_col[:], in_=scale_col[:])
+        nc.vector.tensor_mul(out=scale_col[:], in0=scale_col[:], in1=gain_col[:])
+        nc.vector.tensor_sub(out=shift_col[:], in0=bias_col[:], in1=mean_col[:])
+        nc.vector.tensor_mul(out=shift_col[:], in0=shift_col[:], in1=scale_col[:])
+        nc.vector.tensor_add(out=shift_col[:], in0=shift_col[:], in1=offset_col[:])
+
+        scale_bc = consts.tile([P, FEATURES], F32)
+        shift_bc = consts.tile([P, FEATURES], F32)
+
+        def spread_over_partitions(column, tag):
+            bank = acc_psum.tile([P, BANK], F32, tag=tag, name="spread")
+            for j in range(PER_PARTITION):
+                nc.tensor.transpose(
+                    bank[:, j * P : (j + 1) * P], column[:, j : j + 1].to_broadcast([P, P]), ident[:]
+                )
+            return bank[:].rearrange("m (j p) -> m p j", j=PER_PARTITION)
+
+        factor = consts.tile([P, BLOCKS * FEATURES], F32)
+        addend = consts.tile([P, BLOCKS * FEATURES], F32)
+
+        def prepare_row_block(b):
+            cols = slice(b * FEATURES, (b + 1) * FEATURES)
+            nc.vector.tensor_mul(out=factor[:, cols], in0=scale_bc[:], in1=y_sb[:, cols])
+            nc.vector.tensor_add(out=addend[:, cols], in0=shift_bc[:], in1=y_sb[:, cols])
+            nc.vector.tensor_mul(out=addend[:, cols], in0=addend[:, cols], in1=y_sb[:, cols])
+
+        first_free = sum(widths[:PREFETCH]) // K_PASS
+        prepare_in_round = {first_free + 2 * b: b for b in range(BLOCKS)}
+
+        def transpose_bank(g, j):
+            c, i = home[g]
+            words = staged[c][j // 2][:].bitcast(F32)
+            words_per_block = widths[c] // 2
+            bank = turn_psum.tile([P, BANK], F32, tag="bank")
+            for h in range(2):
+                for u in range(2):
+                    w0 = (2 * (j % 2) + h) * words_per_block + i * WORDS + u * P
+                    q = 2 * h + u
+                    nc.tensor.transpose(bank[:, q * P : (q + 1) * P], words[:, w0 : w0 + P], ident[:])
+            return bank
+
+        def empty_bank(copy, g, j, bank):
+            copy(
+                out=grouped[g][:]
+                .bitcast(F32)[:, j * BANK : (j + 1) * BANK]
+                .rearrange("p (h r u) -> p h r u", h=2, u=2),
+                in_=bank[:].rearrange("p (h u r) -> p h r u", h=2, u=2),
+            )
+
+        def quantise_pass(g):
+            words = code_pool.tile([P, ROWS + FEATURES], U32, align_bytes=64, tag="words")
+            scales = code_pool.tile([P, ROWS + FEATURES], U8, align_bytes=64, tag="scales")
+            nc.vector.quantize_mx(out=words[:].bitcast(FP8X4), scales=scales[:], in_=grouped[g][:])
+            quantised[g] = (words, scales)
+
+        acc = []
+
+        def multiply_pass(g):
+            words, scales = quantised[g]
+            for b in range(BLOCKS):
+                nc.tensor.matmul_mx(
+                    out=acc[b][:],
+                    lhsT=words[:, b * P : (b + 1) * P].bitcast(FP8X4),
+                    lhsT_scale=scales[:, b * P : (b + 1) * P],
+                    rhs=words[:, ROWS : ROWS + FEATURES].bitcast(FP8X4),
+                    rhs_scale=scales[:, ROWS : ROWS + FEATURES],
+                    start=(g == 0),
+                    stop=(g == PASSES - 1),
+                )
+
+        for g in range(PASSES):
+            grouped[g] = group_pool.tile(
+                [P, (ROWS + FEATURES) * PACK], BF16, align_bytes=64, tag="grouped", name="grouped"
+            )
+            banks = [transpose_bank(g, j) for j in range(4)]
+            for j in range(3):
+                empty_bank(nc.scalar.copy, g, j, banks[j])
+            if g >= 1:
+                quantise_pass(g - 1)
+            empty_bank(nc.vector.tensor_copy, g, 3, banks[3])
+
+            if g == 1:
+                nc.scalar.copy(
+                    out=scale_bc[:].rearrange("m (p j) -> m p j", j=PER_PARTITION),
+                    in_=spread_over_partitions(scale_col, "acc0"),
+                )
+                nc.vector.tensor_copy(
+                    out=shift_bc[:].rearrange("m (p j) -> m p j", j=PER_PARTITION),
+                    in_=spread_over_partitions(shift_col, "acc1"),
+                )
+                for b in range(BLOCKS):
+                    acc.append(acc_psum.tile([P, FEATURES], F32, tag="acc%d" % b, name="acc%d" % b))
+            if g in prepare_in_round:
+                prepare_row_block(prepare_in_round[g])
+
+            if g >= LAG:
+                multiply_pass(g - LAG)
+            c, i = home[g]
+            if (i + 1) * K_PASS == widths[c] and c + PREFETCH < len(widths):
+                load_chunk(c + PREFETCH)
+
+        quantise_pass(PASSES - 1)
+        for g in range(PASSES - LAG, PASSES):
+            multiply_pass(g)
+
+        for b in range(BLOCKS):
+            cols = slice(b * FEATURES, (b + 1) * FEATURES)
+            result = result_pool.tile([P, FEATURES], F32)
+            nc.vector.tensor_mul(out=result[:], in0=acc[b][:], in1=factor[:, cols])
+            nc.vector.tensor_add(out=result[:], in0=result[:], in1=addend[:, cols])
+            nc.sync.dma_start(out=out[b * P : (b + 1) * P, :], in_=result[:])

@@ -24,9 +24,13 @@ PASSES = K // K_PASS
 WORDS = K_PASS // 2
 PER_PARTITION = FEATURES // P
 
-CHUNK_MAX = 2048
-PREFETCH = 4
-LAG = 2
+CHUNK_MAX = 1024
+PREFETCH = 6
+ROUND_PASSES = 2
+ROUNDS = PASSES // ROUND_PASSES
+LAG = 1
+PASS_BANKS = 4
+VECTOR_BANK = 2
 
 FLOPS = 2 * ROWS * FEATURES * K
 
@@ -52,10 +56,10 @@ def tile_modelnew_k_kernel(
     with ExitStack() as ctx:
         consts = ctx.enter_context(tc.tile_pool(name="consts", bufs=1))
         stage = ctx.enter_context(tc.tile_pool(name="stage", bufs=PREFETCH))
-        group_pool = ctx.enter_context(tc.tile_pool(name="grouped", bufs=3))
-        code_pool = ctx.enter_context(tc.tile_pool(name="codes", bufs=LAG + 1))
+        group_pool = ctx.enter_context(tc.tile_pool(name="grouped", bufs=2 * ROUND_PASSES))
+        code_pool = ctx.enter_context(tc.tile_pool(name="codes", bufs=(LAG + 1) * ROUND_PASSES))
         result_pool = ctx.enter_context(tc.tile_pool(name="result", bufs=BLOCKS))
-        turn_psum = ctx.enter_context(tc.psum_pool(name="turn", bufs=4))
+        turn_psum = ctx.enter_context(tc.psum_pool(name="turn", bufs=PASS_BANKS))
         acc_psum = ctx.enter_context(tc.psum_pool(name="acc", bufs=1))
         ctx.enter_context(tc.manual_schedule())
 
@@ -125,7 +129,7 @@ def tile_modelnew_k_kernel(
             nc.vector.tensor_add(out=addend[:, cols], in0=shift_bc[:], in1=y_sb[:, cols])
             nc.vector.tensor_mul(out=addend[:, cols], in0=addend[:, cols], in1=y_sb[:, cols])
 
-        first_free = sum(widths[:PREFETCH]) // K_PASS
+        first_free = sum(widths[:PREFETCH]) // (K_PASS * ROUND_PASSES)
         prepare_in_round = {first_free + 2 * b: b for b in range(BLOCKS)}
 
         def transpose_bank(g, j):
@@ -169,18 +173,23 @@ def tile_modelnew_k_kernel(
                     stop=(g == PASSES - 1),
                 )
 
-        for g in range(PASSES):
-            grouped[g] = group_pool.tile(
-                [P, (ROWS + FEATURES) * PACK], BF16, align_bytes=64, tag="grouped", name="grouped"
-            )
-            banks = [transpose_bank(g, j) for j in range(4)]
-            for j in range(3):
-                empty_bank(nc.scalar.copy, g, j, banks[j])
-            if g >= 1:
-                quantise_pass(g - 1)
-            empty_bank(nc.vector.tensor_copy, g, 3, banks[3])
+        for r in range(ROUNDS):
+            for g in range(r * ROUND_PASSES, (r + 1) * ROUND_PASSES):
+                grouped[g] = group_pool.tile(
+                    [P, (ROWS + FEATURES) * PACK], BF16, align_bytes=64, tag="grouped", name="grouped"
+                )
+                banks = [transpose_bank(g, j) for j in range(PASS_BANKS)]
+                for j in range(PASS_BANKS):
+                    if j != VECTOR_BANK:
+                        empty_bank(nc.scalar.copy, g, j, banks[j])
+                if r >= 1:
+                    quantise_pass(g - ROUND_PASSES)
+                empty_bank(nc.vector.tensor_copy, g, VECTOR_BANK, banks[VECTOR_BANK])
+                c, i = home[g]
+                if (i + 1) * K_PASS == widths[c] and c + PREFETCH < len(widths):
+                    load_chunk(c + PREFETCH)
 
-            if g == 1:
+            if r == LAG - 1:
                 nc.scalar.copy(
                     out=scale_bc[:].rearrange("m (p j) -> m p j", j=PER_PARTITION),
                     in_=spread_over_partitions(scale_col, "acc0"),
@@ -191,17 +200,16 @@ def tile_modelnew_k_kernel(
                 )
                 for b in range(BLOCKS):
                     acc.append(acc_psum.tile([P, FEATURES], F32, tag="acc%d" % b, name="acc%d" % b))
-            if g in prepare_in_round:
-                prepare_row_block(prepare_in_round[g])
+            if r in prepare_in_round:
+                prepare_row_block(prepare_in_round[r])
 
-            if g >= LAG:
-                multiply_pass(g - LAG)
-            c, i = home[g]
-            if (i + 1) * K_PASS == widths[c] and c + PREFETCH < len(widths):
-                load_chunk(c + PREFETCH)
+            if r >= LAG:
+                for g in range((r - LAG) * ROUND_PASSES, (r - LAG + 1) * ROUND_PASSES):
+                    multiply_pass(g)
 
-        quantise_pass(PASSES - 1)
-        for g in range(PASSES - LAG, PASSES):
+        for g in range(PASSES - ROUND_PASSES, PASSES):
+            quantise_pass(g)
+        for g in range(PASSES - LAG * ROUND_PASSES, PASSES):
             multiply_pass(g)
 
         for b in range(BLOCKS):

@@ -30,7 +30,6 @@ ROUND_PASSES = 2
 ROUNDS = PASSES // ROUND_PASSES
 LAG = 1
 PASS_BANKS = 4
-VECTOR_BANK = 2
 
 FLOPS = 2 * ROWS * FEATURES * K
 
@@ -174,20 +173,24 @@ def tile_modelnew_k_kernel(
                 )
 
         for r in range(ROUNDS):
-            for g in range(r * ROUND_PASSES, (r + 1) * ROUND_PASSES):
+            round_passes = range(r * ROUND_PASSES, (r + 1) * ROUND_PASSES)
+            for g in round_passes:
                 grouped[g] = group_pool.tile(
                     [P, (ROWS + FEATURES) * PACK], BF16, align_bytes=64, tag="grouped", name="grouped"
                 )
                 banks = [transpose_bank(g, j) for j in range(PASS_BANKS)]
                 for j in range(PASS_BANKS):
-                    if j != VECTOR_BANK:
+                    if g != round_passes[-1] and j % 2 == 1:
+                        empty_bank(nc.vector.tensor_copy, g, j, banks[j])
+                    else:
                         empty_bank(nc.scalar.copy, g, j, banks[j])
-                if r >= 1:
-                    quantise_pass(g - ROUND_PASSES)
-                empty_bank(nc.vector.tensor_copy, g, VECTOR_BANK, banks[VECTOR_BANK])
                 c, i = home[g]
                 if (i + 1) * K_PASS == widths[c] and c + PREFETCH < len(widths):
                     load_chunk(c + PREFETCH)
+            for g in round_passes:
+                if g == round_passes[-1] and r in prepare_in_round:
+                    prepare_row_block(prepare_in_round[r])
+                quantise_pass(g)
 
             if r == LAG - 1:
                 nc.scalar.copy(
@@ -200,21 +203,24 @@ def tile_modelnew_k_kernel(
                 )
                 for b in range(BLOCKS):
                     acc.append(acc_psum.tile([P, FEATURES], F32, tag="acc%d" % b, name="acc%d" % b))
-            if r in prepare_in_round:
-                prepare_row_block(prepare_in_round[r])
 
             if r >= LAG:
                 for g in range((r - LAG) * ROUND_PASSES, (r - LAG + 1) * ROUND_PASSES):
                     multiply_pass(g)
 
-        for g in range(PASSES - ROUND_PASSES, PASSES):
-            quantise_pass(g)
         for g in range(PASSES - LAG * ROUND_PASSES, PASSES):
             multiply_pass(g)
 
+        results = []
         for b in range(BLOCKS):
-            cols = slice(b * FEATURES, (b + 1) * FEATURES)
             result = result_pool.tile([P, FEATURES], F32)
-            nc.vector.tensor_mul(out=result[:], in0=acc[b][:], in1=factor[:, cols])
-            nc.vector.tensor_add(out=result[:], in0=result[:], in1=addend[:, cols])
-            nc.sync.dma_start(out=out[b * P : (b + 1) * P, :], in_=result[:])
+            nc.vector.tensor_mul(
+                out=result[:], in0=acc[b][:], in1=factor[:, b * FEATURES : (b + 1) * FEATURES]
+            )
+            results.append(result)
+        for b in range(BLOCKS):
+            adder = nc.gpsimd if b < BLOCKS // 2 else nc.vector
+            adder.tensor_add(
+                out=results[b][:], in0=results[b][:], in1=addend[:, b * FEATURES : (b + 1) * FEATURES]
+            )
+            nc.sync.dma_start(out=out[b * P : (b + 1) * P, :], in_=results[b][:])

from contextlib import ExitStack

import concourse.mybir as mybir
from concourse.masks import make_identity

F32 = mybir.dt.float32
BF16 = mybir.dt.bfloat16
U32 = mybir.dt.uint32
U8 = mybir.dt.uint8
FP8X4 = mybir.dt.float8_e4m3fn_x4
SQRT = mybir.ActivationFunctionType.Sqrt

P = 128
PACK = 4
K_PASS = P * PACK
BANK = 512

ROWS = 512
FEATURES = 512
K = 16384
EPS = 1e-5
BLOCKS = ROWS // P
PASSES = K // K_PASS
WORDS = K_PASS // 2
PER_PARTITION = FEATURES // P

CHUNK_MAX = 1024
PREFETCH = 6
ROUND_PASSES = 2
ROUNDS = PASSES // ROUND_PASSES
LAG = 1
PASS_BANKS = 4

FLOPS = 2 * ROWS * FEATURES * K


def chunk_widths():
    widths = [K_PASS]
    while sum(widths) < K:
        widths.append(min(sum(widths), CHUNK_MAX))
    assert sum(widths) == K
    return widths


def tile_modelnew_k_kernel(
    tc, x, y, weight, bias, running_mean, running_var, norm_weight, norm_bias, out
):
    nc = tc.nc
    widths = chunk_widths()
    home = [(c, i) for c, width in enumerate(widths) for i in range(width // K_PASS)]
    x_view = x.rearrange("(b p) k -> p b k", p=P)
    w_view = weight.rearrange("(b p) k -> p b k", p=P)
    y_view = y.rearrange("(b p) n -> p b n", p=P)

    with ExitStack() as ctx:
        consts = ctx.enter_context(tc.tile_pool(name="consts", bufs=1))
        stage = ctx.enter_context(tc.tile_pool(name="stage", bufs=PREFETCH))
        group_pool = ctx.enter_context(tc.tile_pool(name="grouped", bufs=2 * ROUND_PASSES))
        code_pool = ctx.enter_context(tc.tile_pool(name="codes", bufs=(LAG + 1) * ROUND_PASSES))
        result_pool = ctx.enter_context(tc.tile_pool(name="result", bufs=BLOCKS))
        turn_psum = ctx.enter_context(tc.psum_pool(name="turn", bufs=PASS_BANKS))
        acc_psum = ctx.enter_context(tc.psum_pool(name="acc", bufs=1))
        ctx.enter_context(tc.manual_schedule())

        staged = {}
        grouped = {}
        quantised = {}

        def load_chunk(c):
            k0, width = sum(widths[:c]), widths[c]
            x_st = stage.tile([P, BLOCKS * width], BF16, tag="x_st")
            nc.sync.dma_start(
                out=x_st[:].rearrange("p (b k) -> p b k", b=BLOCKS),
                in_=x_view[:, :, k0 : k0 + width],
            )
            w_st = stage.tile([P, BLOCKS * width], BF16, tag="w_st")
            nc.sync.dma_start(
                out=w_st[:].rearrange("p (b k) -> p b k", b=BLOCKS),
                in_=w_view[:, :, k0 : k0 + width],
            )
            staged[c] = (x_st, w_st)

        def load_vector(vector, name):
            column = consts.tile([P, PER_PARTITION], BF16, name=name)
            nc.scalar.dma_start(out=column[:], in_=vector.rearrange("(p j) -> p j", j=PER_PARTITION))
            return column

        var_col = load_vector(running_var, "var_col")
        gain_col = load_vector(norm_weight, "gain_col")
        bias_col = load_vector(bias, "bias_col")
        mean_col = load_vector(running_mean, "mean_col")
        offset_col = load_vector(norm_bias, "offset_col")

        for c in range(PREFETCH):
            load_chunk(c)
        y_sb = consts.tile([P, BLOCKS * FEATURES], BF16)
        nc.sync.dma_start(out=y_sb[:].rearrange("p (b n) -> p b n", b=BLOCKS), in_=y_view)

        ident = consts.tile([P, P], F32)
        make_identity(nc, ident[:])

        scale_col = consts.tile([P, PER_PARTITION], F32)
        shift_col = consts.tile([P, PER_PARTITION], F32)
        nc.scalar.activation(out=scale_col[:], in_=var_col[:], func=SQRT, bias=EPS)
        nc.vector.reciprocal(out=scale_col[:], in_=scale_col[:])
        nc.vector.tensor_mul(out=scale_col[:], in0=scale_col[:], in1=gain_col[:])
        nc.vector.tensor_sub(out=shift_col[:], in0=bias_col[:], in1=mean_col[:])
        nc.vector.tensor_mul(out=shift_col[:], in0=shift_col[:], in1=scale_col[:])
        nc.vector.tensor_add(out=shift_col[:], in0=shift_col[:], in1=offset_col[:])

        scale_bc = consts.tile([P, FEATURES], F32)
        shift_bc = consts.tile([P, FEATURES], F32)

        def spread_over_partitions(column, tag):
            bank = acc_psum.tile([P, BANK], F32, tag=tag, name="spread")
            for j in range(PER_PARTITION):
                nc.tensor.transpose(
                    bank[:, j * P : (j + 1) * P], column[:, j : j + 1].to_broadcast([P, P]), ident[:]
                )
            return bank[:].rearrange("m (j p) -> m p j", j=PER_PARTITION)

        factor = consts.tile([P, BLOCKS * FEATURES], F32)
        addend = consts.tile([P, BLOCKS * FEATURES], F32)

        def prepare_row_block(b):
            cols = slice(b * FEATURES, (b + 1) * FEATURES)
            nc.vector.tensor_mul(out=factor[:, cols], in0=scale_bc[:], in1=y_sb[:, cols])
            nc.vector.tensor_add(out=addend[:, cols], in0=shift_bc[:], in1=y_sb[:, cols])
            nc.vector.tensor_mul(out=addend[:, cols], in0=addend[:, cols], in1=y_sb[:, cols])

        first_free = sum(widths[:PREFETCH]) // (K_PASS * ROUND_PASSES)
        prepare_in_round = {first_free + 2 * b: b for b in range(BLOCKS)}

        def transpose_bank(g, j):
            c, i = home[g]
            words = staged[c][j // 2][:].bitcast(F32)
            words_per_block = widths[c] // 2
            bank = turn_psum.tile([P, BANK], F32, tag="bank")
            for h in range(2):
                for u in range(2):
                    w0 = (2 * (j % 2) + h) * words_per_block + i * WORDS + u * P
                    q = 2 * h + u
                    nc.tensor.transpose(bank[:, q * P : (q + 1) * P], words[:, w0 : w0 + P], ident[:])
            return bank

        def empty_bank(copy, g, j, bank):
            copy(
                out=grouped[g][:]
                .bitcast(F32)[:, j * BANK : (j + 1) * BANK]
                .rearrange("p (h r u) -> p h r u", h=2, u=2),
                in_=bank[:].rearrange("p (h u r) -> p h r u", h=2, u=2),
            )

        def quantise_pass(g):
            words = code_pool.tile([P, ROWS + FEATURES], U32, align_bytes=64, tag="words")
            scales = code_pool.tile([P, ROWS + FEATURES], U8, align_bytes=64, tag="scales")
            nc.vector.quantize_mx(out=words[:].bitcast(FP8X4), scales=scales[:], in_=grouped[g][:])
            quantised[g] = (words, scales)

        acc = []

        def multiply_pass(g):
            words, scales = quantised[g]
            for b in range(BLOCKS):
                nc.tensor.matmul_mx(
                    out=acc[b][:],
                    lhsT=words[:, b * P : (b + 1) * P].bitcast(FP8X4),
                    lhsT_scale=scales[:, b * P : (b + 1) * P],
                    rhs=words[:, ROWS : ROWS + FEATURES].bitcast(FP8X4),
                    rhs_scale=scales[:, ROWS : ROWS + FEATURES],
                    start=(g == 0),
                    stop=(g == PASSES - 1),
                )

        for r in range(ROUNDS):
            round_passes = range(r * ROUND_PASSES, (r + 1) * ROUND_PASSES)
            for g in round_passes:
                grouped[g] = group_pool.tile(
                    [P, (ROWS + FEATURES) * PACK], BF16, align_bytes=64, tag="grouped", name="grouped"
                )
                banks = [transpose_bank(g, j) for j in range(PASS_BANKS)]
                for j in range(PASS_BANKS):
                    if g != round_passes[-1] and j % 2 == 1:
                        empty_bank(nc.vector.tensor_copy, g, j, banks[j])
                    else:
                        empty_bank(nc.scalar.copy, g, j, banks[j])
                c, i = home[g]
                if (i + 1) * K_PASS == widths[c] and c + PREFETCH < len(widths):
                    load_chunk(c + PREFETCH)
            for g in round_passes:
                if g == round_passes[-1] and r in prepare_in_round:
                    prepare_row_block(prepare_in_round[r])
                quantise_pass(g)

            if r == LAG - 1:
                nc.scalar.copy(
                    out=scale_bc[:].rearrange("m (p j) -> m p j", j=PER_PARTITION),
                    in_=spread_over_partitions(scale_col, "acc0"),
                )
                nc.vector.tensor_copy(
                    out=shift_bc[:].rearrange("m (p j) -> m p j", j=PER_PARTITION),
                    in_=spread_over_partitions(shift_col, "acc1"),
                )
                for b in range(BLOCKS):
                    acc.append(acc_psum.tile([P, FEATURES], F32, tag="acc%d" % b, name="acc%d" % b))

            if r >= LAG:
                for g in range((r - LAG) * ROUND_PASSES, (r - LAG + 1) * ROUND_PASSES):
                    multiply_pass(g)

        for g in range(PASSES - LAG * ROUND_PASSES, PASSES):
            multiply_pass(g)

        results = []
        for b in range(BLOCKS):
            result = result_pool.tile([P, FEATURES], F32)
            nc.vector.tensor_mul(
                out=result[:], in0=acc[b][:], in1=factor[:, b * FEATURES : (b + 1) * FEATURES]
            )
            results.append(result)
        for b in range(BLOCKS):
            adder = nc.gpsimd if b < BLOCKS // 2 else nc.vector
            adder.tensor_add(
                out=results[b][:], in0=results[b][:], in1=addend[:, b * FEATURES : (b + 1) * FEATURES]
            )
            nc.sync.dma_start(out=out[b * P : (b + 1) * P, :], in_=results[b][:])
